import numpy as np
import ml_dtypes

BF16 = ml_dtypes.bfloat16


def bf(x):
    return np.asarray(x, np.float32).astype(BF16)


def f32(x):
    return np.asarray(x, np.float32)


def f64(x):
    return np.asarray(x).astype(np.float64)


def striped(idx):
    return np.tile(idx.reshape(-1, 16).T, (8, 1))


D, S, R, L, B, N, Q, T = 128, 1024, 128, 16, 128, 2048, 4, 3


def setup_inputs():
    return {
        "table": bf(np.random.standard_normal((D, S))),
        "w_down": bf(np.random.standard_normal((D, R)) / np.sqrt(D)),
        "w_re": bf(np.random.standard_normal((T * Q * R, R)) / np.sqrt(T * Q * R)),
        "b_re": f32(0.1 * np.random.standard_normal((R, 1))),
        "offs": striped(np.random.permutation(np.tile(np.arange(S), 2))[:N]),
    }


def reference(table, w_down, w_re, b_re, offs):
    idx = offs[:16].T.reshape(-1)
    tok = (f64(w_down).T @ f64(table)[:, idx]).reshape(R, B, L)
    mean = tok.sum(axis=2) / L
    sq = (tok * tok).sum(axis=2) / L
    sd = np.sqrt(sq - mean * mean)
    feat = np.concatenate([mean, tok.max(axis=2), tok.min(axis=2), sd], axis=0)
    res = np.tile(feat, (T, 1)).T @ f64(w_re) + f64(b_re).T
    return res / np.sqrt((res * res).sum(axis=1, keepdims=True))

@@ -1,0 +1,97 @@
+import concourse.mybir as mybir
+
+F32 = mybir.dt.float32
+BF16 = mybir.dt.bfloat16
+U16 = mybir.dt.uint16
+ALU = mybir.AluOpType
+ACT = mybir.ActivationFunctionType
+X = mybir.AxisListType.X
+
+P = 128
+S = 1024
+N = 2048
+L = 16
+B = N // L
+R = 128
+PIECE = 512
+PIECES = N // PIECE
+E = PIECE // L
+AGGS = 4
+SCALERS = 3
+
+FLOPS = 2 * P * R * N + 2 * SCALERS * AGGS * R * B * R
+
+
+def tile_basepnaretriever_kernel(tc, table, w_down, w_re, b_re, offs, out):
+    nc = tc.nc
+    with (
+        tc.tile_pool(name="held", bufs=1) as held,
+        tc.psum_pool(name="psum", bufs=1) as psum,
+    ):
+        offsets = held.tile([P, N // 16], U16, name="offsets")
+        nc.sync.dma_start(offsets[:], offs)
+        table_sb = held.tile([P, S], BF16, name="table_sb")
+        nc.scalar.dma_start(table_sb[:], table)
+        w_down_sb = held.tile([P, R], BF16, name="w_down_sb")
+        nc.sync.dma_start(w_down_sb[:], w_down)
+        w_re_sb = held.tile([P, SCALERS * AGGS, R], BF16, name="w_re_sb")
+        nc.sync.dma_start(w_re_sb[:], w_re.rearrange("(c f) r -> f c r", f=P))
+        bias_sb = held.tile([P, R], F32, name="bias_sb")
+        nc.scalar.dma_start(bias_sb[:], b_re.rearrange("r o -> (r o)").partition_broadcast(P))
+
+        tok_sum = held.tile([P, B], F32, name="tok_sum")
+        sq_sum = held.tile([P, B], F32, name="sq_sum")
+        feat = [held.tile([P, B], BF16, name=f"feat{a}") for a in range(AGGS)]
+        mean_bf, max_bf, min_bf, sd_bf = feat
+
+        for piece in range(PIECES):
+            tok = psum.tile([P, PIECE], F32, name=f"tok{piece}")
+            picked = table_sb[:].indirect(offsets[:, piece * E : (piece + 1) * E])
+            nc.tensor.matmul(tok[:], w_down_sb[:], picked, start=True, stop=True)
+
+            by_entity = tok[:].rearrange("r (e t) -> r e t", t=L)
+            ents = slice(piece * E, (piece + 1) * E)
+            squares = held.tile([P, PIECE], F32, name=f"squares{piece}")
+            nc.scalar.activation(squares[:], tok[:], ACT.Square)
+            nc.vector.tensor_reduce(tok_sum[:, ents], by_entity, X, ALU.add)
+            nc.vector.tensor_reduce(
+                sq_sum[:, ents], squares[:].rearrange("r (e t) -> r e t", t=L), X, ALU.add
+            )
+            with nc.allow_low_precision(reason="max and min only pick an element"):
+                nc.vector.tensor_reduce(max_bf[:, ents], by_entity, X, ALU.max)
+                nc.vector.tensor_reduce(min_bf[:, ents], by_entity, X, ALU.min)
+
+        nc.scalar.activation(mean_bf[:], tok_sum[:], ACT.Copy, scale=1.0 / L)
+        sum_squared = held.tile([P, B], F32, name="sum_squared")
+        nc.vector.tensor_tensor(sum_squared[:], tok_sum[:], tok_sum[:], ALU.mult)
+        raised = held.tile([P, B], F32, name="raised")
+        nc.vector.scalar_tensor_tensor(
+            raised[:], sq_sum[:], float(L), sum_squared[:], ALU.mult, ALU.max
+        )
+        spread = held.tile([P, B], F32, name="spread")
+        nc.vector.tensor_tensor(spread[:], raised[:], sum_squared[:], ALU.subtract)
+        nc.scalar.activation(sd_bf[:], spread[:], ACT.Sqrt, scale=1.0 / (L * L))
+
+        res_ps = psum.tile([P, R], F32, name="res_ps")
+        blocks = [(a, t) for a in range(AGGS) for t in range(SCALERS)]
+        for i, (a, t) in enumerate(blocks):
+            nc.tensor.matmul(
+                res_ps[:],
+                feat[a][:],
+                w_re_sb[:, t * AGGS + a, :],
+                start=(i == 0),
+                stop=(i == len(blocks) - 1),
+            )
+
+        res = held.tile([P, R], F32, name="res")
+        nc.vector.tensor_tensor(res[:], res_ps[:], bias_sb[:], ALU.add)
+        res_squared = held.tile([P, R], F32, name="res_squared")
+        length2 = held.tile([P, 1], F32, name="length2")
+        nc.scalar.activation(res_squared[:], res[:], ACT.Square, accum_out=length2[:])
+        length = held.tile([P, 1], F32, name="length")
+        nc.scalar.activation(length[:], length2[:], ACT.Sqrt)
+        inv_length = held.tile([P, 1], F32, name="inv_length")
+        nc.vector.reciprocal(inv_length[:], length[:])
+        unit = held.tile([P, R], F32, name="unit")
+        nc.vector.tensor_scalar(unit[:], res[:], inv_length[:], None, ALU.mult)
+        nc.sync.dma_start(out, unit[:])

@@ -20,6 +20,8 @@ AGGS = 4
 SCALERS = 3
 
 FLOPS = 2 * P * R * N + 2 * SCALERS * AGGS * R * B * R
+HALF = N // 2
+HALVES = N // HALF
 
 
 def tile_basepnaretriever_kernel(tc, table, w_down, w_re, b_re, offs, out):
@@ -36,62 +38,90 @@ def tile_basepnaretriever_kernel(tc, table, w_down, w_re, b_re, offs, out):
         nc.sync.dma_start(w_down_sb[:], w_down)
         w_re_sb = held.tile([P, SCALERS * AGGS, R], BF16, name="w_re_sb")
         nc.sync.dma_start(w_re_sb[:], w_re.rearrange("(c f) r -> f c r", f=P))
-        bias_sb = held.tile([P, R], F32, name="bias_sb")
-        nc.scalar.dma_start(bias_sb[:], b_re.rearrange("r o -> (r o)").partition_broadcast(P))
+        bias_rows = held.tile([P, R], F32, name="bias_rows")
+        nc.gpsimd.memset(bias_rows[:], 0.0)
+        nc.sync.dma_start(bias_rows[0:1, :], b_re.rearrange("r o -> o r"))
+        ones = held.tile([P, B], F32, name="ones")
+        nc.gpsimd.memset(ones[:], 1.0)
+
+        warm = held.tile([P, 1], F32, name="warm")
+        nc.scalar.activation(warm[:], ones[:, 0:1], ACT.Sqrt)
 
         tok_sum = held.tile([P, B], F32, name="tok_sum")
         sq_sum = held.tile([P, B], F32, name="sq_sum")
+        tok_bf = held.tile([P, N], BF16, name="tok_bf")
         feat = [held.tile([P, B], BF16, name=f"feat{a}") for a in range(AGGS)]
         mean_bf, max_bf, min_bf, sd_bf = feat
 
+        toks = []
         for piece in range(PIECES):
             tok = psum.tile([P, PIECE], F32, name=f"tok{piece}")
             picked = table_sb[:].indirect(offsets[:, piece * E : (piece + 1) * E])
             nc.tensor.matmul(tok[:], w_down_sb[:], picked, start=True, stop=True)
+            toks.append(tok)
+        res_ps = psum.tile([P, R], F32, name="res_ps")
+        nc.tensor.matmul(res_ps[:], ones[:], bias_rows[:], start=True, stop=False)
 
-            by_entity = tok[:].rearrange("r (e t) -> r e t", t=L)
+        def sums(piece):
             ents = slice(piece * E, (piece + 1) * E)
+            tok = toks[piece]
+            nc.vector.tensor_reduce(
+                tok_sum[:, ents], tok[:].rearrange("r (e t) -> r e t", t=L), X, ALU.add
+            )
             squares = held.tile([P, PIECE], F32, name=f"squares{piece}")
             nc.scalar.activation(squares[:], tok[:], ACT.Square)
-            nc.vector.tensor_reduce(tok_sum[:, ents], by_entity, X, ALU.add)
+            nc.scalar.activation(tok_bf[:, piece * PIECE : (piece + 1) * PIECE], tok[:], ACT.Copy)
             nc.vector.tensor_reduce(
                 sq_sum[:, ents], squares[:].rearrange("r (e t) -> r e t", t=L), X, ALU.add
             )
-            with nc.allow_low_precision(reason="max and min only pick an element"):
-                nc.vector.tensor_reduce(max_bf[:, ents], by_entity, X, ALU.max)
-                nc.vector.tensor_reduce(min_bf[:, ents], by_entity, X, ALU.min)
+
+        def extreme(half, op, result, label):
+            ents = HALF // L
+            cur = tok_bf[:, half * HALF : (half + 1) * HALF].rearrange("r (e t) -> r e t", t=L)
+            width = L // 2
+            while width > 1:
+                nxt = held.tile([P, ents, width], BF16, name=f"{label}{half}_{width}")
+                nc.vector.tensor_tensor(nxt[:], cur[:, :, 0:width], cur[:, :, width : 2 * width], op)
+                cur = nxt[:]
+                width //= 2
+            last = result[:, half * ents : (half + 1) * ents].unsqueeze(2)
+            nc.vector.tensor_tensor(last, cur[:, :, 0:1], cur[:, :, 1:2], op)
+
+        sums(0)
+        sums(1)
+        extreme(0, ALU.max, max_bf, "max")
+        extreme(0, ALU.min, min_bf, "min")
+        sums(2)
+        sums(3)
 
         nc.scalar.activation(mean_bf[:], tok_sum[:], ACT.Copy, scale=1.0 / L)
-        sum_squared = held.tile([P, B], F32, name="sum_squared")
-        nc.vector.tensor_tensor(sum_squared[:], tok_sum[:], tok_sum[:], ALU.mult)
-        raised = held.tile([P, B], F32, name="raised")
-        nc.vector.scalar_tensor_tensor(
-            raised[:], sq_sum[:], float(L), sum_squared[:], ALU.mult, ALU.max
-        )
+        sum2_over_l = held.tile([P, B], F32, name="sum2_over_l")
+        nc.scalar.activation(sum2_over_l[:], tok_sum[:], ACT.Square, scale=0.25)
         spread = held.tile([P, B], F32, name="spread")
-        nc.vector.tensor_tensor(spread[:], raised[:], sum_squared[:], ALU.subtract)
-        nc.scalar.activation(sd_bf[:], spread[:], ACT.Sqrt, scale=1.0 / (L * L))
+        nc.vector.tensor_tensor(spread[:], sq_sum[:], sum2_over_l[:], ALU.max)
+        nc.vector.tensor_tensor(spread[:], spread[:], sum2_over_l[:], ALU.subtract)
+        nc.scalar.activation(sd_bf[:], spread[:], ACT.Sqrt, scale=1.0 / L)
 
-        res_ps = psum.tile([P, R], F32, name="res_ps")
-        blocks = [(a, t) for a in range(AGGS) for t in range(SCALERS)]
+        extreme(1, ALU.max, max_bf, "max")
+        extreme(1, ALU.min, min_bf, "min")
+
+        blocks = [(a, t) for a in (0, 3, 1, 2) for t in range(SCALERS)]
         for i, (a, t) in enumerate(blocks):
             nc.tensor.matmul(
                 res_ps[:],
                 feat[a][:],
                 w_re_sb[:, t * AGGS + a, :],
-                start=(i == 0),
+                start=False,
                 stop=(i == len(blocks) - 1),
             )
 
-        res = held.tile([P, R], F32, name="res")
-        nc.vector.tensor_tensor(res[:], res_ps[:], bias_sb[:], ALU.add)
         res_squared = held.tile([P, R], F32, name="res_squared")
         length2 = held.tile([P, 1], F32, name="length2")
-        nc.scalar.activation(res_squared[:], res[:], ACT.Square, accum_out=length2[:])
+        nc.scalar.activation(res_squared[:], res_ps[:], ACT.Square, accum_out=length2[:])
         length = held.tile([P, 1], F32, name="length")
         nc.scalar.activation(length[:], length2[:], ACT.Sqrt)
         inv_length = held.tile([P, 1], F32, name="inv_length")
         nc.vector.reciprocal(inv_length[:], length[:])
         unit = held.tile([P, R], F32, name="unit")
-        nc.vector.tensor_scalar(unit[:], res[:], inv_length[:], None, ALU.mult)
+        nc.vector.tensor_scalar(unit[:], res_ps[:], inv_length[:], None, ALU.mult)
         nc.sync.dma_start(out, unit[:])

@@ -22,6 +22,9 @@ SCALERS = 3
 FLOPS = 2 * P * R * N + 2 * SCALERS * AGGS * R * B * R
 HALF = N // 2
 HALVES = N // HALF
+PIECES_IN_HALF = HALF // PIECE
+EH = HALF // L
+WARM_UPS = 5
 
 
 def tile_basepnaretriever_kernel(tc, table, w_down, w_re, b_re, offs, out):
@@ -37,7 +40,7 @@ def tile_basepnaretriever_kernel(tc, table, w_down, w_re, b_re, offs, out):
         w_down_sb = held.tile([P, R], BF16, name="w_down_sb")
         nc.sync.dma_start(w_down_sb[:], w_down)
         w_re_sb = held.tile([P, SCALERS * AGGS, R], BF16, name="w_re_sb")
-        nc.sync.dma_start(w_re_sb[:], w_re.rearrange("(c f) r -> f c r", f=P))
+        nc.scalar.dma_start(w_re_sb[:], w_re.rearrange("(c f) r -> f c r", f=P))
         bias_rows = held.tile([P, R], F32, name="bias_rows")
         nc.gpsimd.memset(bias_rows[:], 0.0)
         nc.sync.dma_start(bias_rows[0:1, :], b_re.rearrange("r o -> o r"))
@@ -47,11 +50,19 @@ def tile_basepnaretriever_kernel(tc, table, w_down, w_re, b_re, offs, out):
         warm = held.tile([P, 1], F32, name="warm")
         nc.scalar.activation(warm[:], ones[:, 0:1], ACT.Sqrt)
 
+        zeros = held.tile([P, PIECE], BF16, name="zeros")
+        nc.vector.memset(zeros[:], 0.0)
+        idle_ps = psum.tile([P, PIECE], F32, name="idle_ps")
+        for i in range(WARM_UPS):
+            nc.tensor.matmul(idle_ps[:], zeros[:, 0:P], zeros[:], start=True, stop=True)
+
         tok_sum = held.tile([P, B], F32, name="tok_sum")
         sq_sum = held.tile([P, B], F32, name="sq_sum")
-        tok_bf = held.tile([P, N], BF16, name="tok_bf")
         feat = [held.tile([P, B], BF16, name=f"feat{a}") for a in range(AGGS)]
         mean_bf, max_bf, min_bf, sd_bf = feat
+
+        def by_entity(ap):
+            return ap.rearrange("r (e t) -> r e t", t=L)
 
         toks = []
         for piece in range(PIECES):
@@ -62,37 +73,36 @@ def tile_basepnaretriever_kernel(tc, table, w_down, w_re, b_re, offs, out):
         res_ps = psum.tile([P, R], F32, name="res_ps")
         nc.tensor.matmul(res_ps[:], ones[:], bias_rows[:], start=True, stop=False)
 
-        def sums(piece):
-            ents = slice(piece * E, (piece + 1) * E)
-            tok = toks[piece]
+        for piece in range(PIECES):
             nc.vector.tensor_reduce(
-                tok_sum[:, ents], tok[:].rearrange("r (e t) -> r e t", t=L), X, ALU.add
+                tok_sum[:, piece * E : (piece + 1) * E], by_entity(toks[piece][:]), X, ALU.add
             )
-            squares = held.tile([P, PIECE], F32, name=f"squares{piece}")
-            nc.scalar.activation(squares[:], tok[:], ACT.Square)
-            nc.scalar.activation(tok_bf[:, piece * PIECE : (piece + 1) * PIECE], tok[:], ACT.Copy)
+        squares = [held.tile([P, HALF], F32, name=f"squares{half}") for half in range(HALVES)]
+        tok_bf = [held.tile([P, HALF], BF16, name=f"tok_bf{half}") for half in range(HALVES)]
+        for func, dest in ((ACT.Square, squares), (ACT.Copy, tok_bf)):
+            for piece in range(PIECES):
+                half, part = divmod(piece, PIECES_IN_HALF)
+                cols = slice(part * PIECE, (part + 1) * PIECE)
+                nc.scalar.activation(dest[half][:, cols], toks[piece][:], func)
+
+        def sum_of_squares(half):
             nc.vector.tensor_reduce(
-                sq_sum[:, ents], squares[:].rearrange("r (e t) -> r e t", t=L), X, ALU.add
+                sq_sum[:, half * EH : (half + 1) * EH], by_entity(squares[half][:]), X, ALU.add
             )
 
         def extreme(half, op, result, label):
-            ents = HALF // L
-            cur = tok_bf[:, half * HALF : (half + 1) * HALF].rearrange("r (e t) -> r e t", t=L)
+            cur = by_entity(tok_bf[half][:])
             width = L // 2
             while width > 1:
-                nxt = held.tile([P, ents, width], BF16, name=f"{label}{half}_{width}")
+                nxt = held.tile([P, EH, width], BF16, name=f"{label}{half}_{width}")
                 nc.vector.tensor_tensor(nxt[:], cur[:, :, 0:width], cur[:, :, width : 2 * width], op)
                 cur = nxt[:]
                 width //= 2
-            last = result[:, half * ents : (half + 1) * ents].unsqueeze(2)
+            last = result[:, half * EH : (half + 1) * EH].unsqueeze(2)
             nc.vector.tensor_tensor(last, cur[:, :, 0:1], cur[:, :, 1:2], op)
 
-        sums(0)
-        sums(1)
-        extreme(0, ALU.max, max_bf, "max")
-        extreme(0, ALU.min, min_bf, "min")
-        sums(2)
-        sums(3)
+        sum_of_squares(0)
+        sum_of_squares(1)
 
         nc.scalar.activation(mean_bf[:], tok_sum[:], ACT.Copy, scale=1.0 / L)
         sum2_over_l = held.tile([P, B], F32, name="sum2_over_l")
@@ -102,8 +112,9 @@ def tile_basepnaretriever_kernel(tc, table, w_down, w_re, b_re, offs, out):
         nc.vector.tensor_tensor(spread[:], spread[:], sum2_over_l[:], ALU.subtract)
         nc.scalar.activation(sd_bf[:], spread[:], ACT.Sqrt, scale=1.0 / L)
 
-        extreme(1, ALU.max, max_bf, "max")
-        extreme(1, ALU.min, min_bf, "min")
+        for op, result, label in ((ALU.max, max_bf, "max"), (ALU.min, min_bf, "min")):
+            for half in range(HALVES):
+                extreme(half, op, result, label)
 
         blocks = [(a, t) for a in (0, 3, 1, 2) for t in range(SCALERS)]
         for i, (a, t) in enumerate(blocks):

@@ -24,7 +24,6 @@ HALF = N // 2
 HALVES = N // HALF
 PIECES_IN_HALF = HALF // PIECE
 EH = HALF // L
-WARM_UPS = 5
 
 
 def tile_basepnaretriever_kernel(tc, table, w_down, w_re, b_re, offs, out):
@@ -49,12 +48,6 @@ def tile_basepnaretriever_kernel(tc, table, w_down, w_re, b_re, offs, out):
 
         warm = held.tile([P, 1], F32, name="warm")
         nc.scalar.activation(warm[:], ones[:, 0:1], ACT.Sqrt)
-
-        zeros = held.tile([P, PIECE], BF16, name="zeros")
-        nc.vector.memset(zeros[:], 0.0)
-        idle_ps = psum.tile([P, PIECE], F32, name="idle_ps")
-        for i in range(WARM_UPS):
-            nc.tensor.matmul(idle_ps[:], zeros[:, 0:P], zeros[:], start=True, stop=True)
 
         tok_sum = held.tile([P, B], F32, name="tok_sum")
         sq_sum = held.tile([P, B], F32, name="sq_sum")
@@ -90,17 +83,6 @@ def tile_basepnaretriever_kernel(tc, table, w_down, w_re, b_re, offs, out):
                 sq_sum[:, half * EH : (half + 1) * EH], by_entity(squares[half][:]), X, ALU.add
             )
 
-        def extreme(half, op, result, label):
-            cur = by_entity(tok_bf[half][:])
-            width = L // 2
-            while width > 1:
-                nxt = held.tile([P, EH, width], BF16, name=f"{label}{half}_{width}")
-                nc.vector.tensor_tensor(nxt[:], cur[:, :, 0:width], cur[:, :, width : 2 * width], op)
-                cur = nxt[:]
-                width //= 2
-            last = result[:, half * EH : (half + 1) * EH].unsqueeze(2)
-            nc.vector.tensor_tensor(last, cur[:, :, 0:1], cur[:, :, 1:2], op)
-
         sum_of_squares(0)
         sum_of_squares(1)
 
@@ -112,9 +94,24 @@ def tile_basepnaretriever_kernel(tc, table, w_down, w_re, b_re, offs, out):
         nc.vector.tensor_tensor(spread[:], spread[:], sum2_over_l[:], ALU.subtract)
         nc.scalar.activation(sd_bf[:], spread[:], ACT.Sqrt, scale=1.0 / L)
 
-        for op, result, label in ((ALU.max, max_bf, "max"), (ALU.min, min_bf, "min")):
-            for half in range(HALVES):
-                extreme(half, op, result, label)
+        chains = [
+            (op, result, label, half)
+            for half in range(HALVES)
+            for op, result, label in ((ALU.max, max_bf, "max"), (ALU.min, min_bf, "min"))
+        ]
+        cur = [by_entity(tok_bf[half][:]) for op, result, label, half in chains]
+        width = L // 2
+        while width >= 1:
+            for c, (op, result, label, half) in enumerate(chains):
+                if width > 1:
+                    nxt = held.tile([P, EH, width], BF16, name=f"{label}{half}_{width}")[:]
+                else:
+                    nxt = result[:, half * EH : (half + 1) * EH].unsqueeze(2)
+                nc.vector.tensor_tensor(
+                    nxt, cur[c][:, :, 0:width], cur[c][:, :, width : 2 * width], op
+                )
+                cur[c] = nxt
+            width //= 2
 
         blocks = [(a, t) for a in (0, 3, 1, 2) for t in range(SCALERS)]
         for i, (a, t) in enumerate(blocks):

@@ -22,8 +22,6 @@ SCALERS = 3
 FLOPS = 2 * P * R * N + 2 * SCALERS * AGGS * R * B * R
 HALF = N // 2
 HALVES = N // HALF
-PIECES_IN_HALF = HALF // PIECE
-EH = HALF // L
 
 
 def tile_basepnaretriever_kernel(tc, table, w_down, w_re, b_re, offs, out):
@@ -39,23 +37,21 @@ def tile_basepnaretriever_kernel(tc, table, w_down, w_re, b_re, offs, out):
         w_down_sb = held.tile([P, R], BF16, name="w_down_sb")
         nc.sync.dma_start(w_down_sb[:], w_down)
         w_re_sb = held.tile([P, SCALERS * AGGS, R], BF16, name="w_re_sb")
-        nc.scalar.dma_start(w_re_sb[:], w_re.rearrange("(c f) r -> f c r", f=P))
+        nc.sync.dma_start(w_re_sb[:], w_re.rearrange("(c f) r -> f c r", f=P))
         bias_rows = held.tile([P, R], F32, name="bias_rows")
         nc.gpsimd.memset(bias_rows[:], 0.0)
         nc.sync.dma_start(bias_rows[0:1, :], b_re.rearrange("r o -> o r"))
         ones = held.tile([P, B], F32, name="ones")
         nc.gpsimd.memset(ones[:], 1.0)
 
-        warm = held.tile([P, 1], F32, name="warm")
-        nc.scalar.activation(warm[:], ones[:, 0:1], ACT.Sqrt)
+        first_set = held.tile([P, 1], F32, name="first_set")
+        nc.scalar.activation(first_set[:], ones[:, 0:1], ACT.Sqrt)
 
         tok_sum = held.tile([P, B], F32, name="tok_sum")
         sq_sum = held.tile([P, B], F32, name="sq_sum")
+        tok_bf = held.tile([P, N], BF16, name="tok_bf")
         feat = [held.tile([P, B], BF16, name=f"feat{a}") for a in range(AGGS)]
         mean_bf, max_bf, min_bf, sd_bf = feat
-
-        def by_entity(ap):
-            return ap.rearrange("r (e t) -> r e t", t=L)
 
         toks = []
         for piece in range(PIECES):
@@ -66,52 +62,53 @@ def tile_basepnaretriever_kernel(tc, table, w_down, w_re, b_re, offs, out):
         res_ps = psum.tile([P, R], F32, name="res_ps")
         nc.tensor.matmul(res_ps[:], ones[:], bias_rows[:], start=True, stop=False)
 
-        for piece in range(PIECES):
+        def sums(piece):
+            ents = slice(piece * E, (piece + 1) * E)
+            tok = toks[piece]
             nc.vector.tensor_reduce(
-                tok_sum[:, piece * E : (piece + 1) * E], by_entity(toks[piece][:]), X, ALU.add
+                tok_sum[:, ents], tok[:].rearrange("r (e t) -> r e t", t=L), X, ALU.add
             )
-        squares = [held.tile([P, HALF], F32, name=f"squares{half}") for half in range(HALVES)]
-        tok_bf = [held.tile([P, HALF], BF16, name=f"tok_bf{half}") for half in range(HALVES)]
-        for func, dest in ((ACT.Square, squares), (ACT.Copy, tok_bf)):
-            for piece in range(PIECES):
-                half, part = divmod(piece, PIECES_IN_HALF)
-                cols = slice(part * PIECE, (part + 1) * PIECE)
-                nc.scalar.activation(dest[half][:, cols], toks[piece][:], func)
-
-        def sum_of_squares(half):
+            squares = held.tile([P, PIECE], F32, name=f"squares{piece}")
+            nc.scalar.activation(squares[:], tok[:], ACT.Square)
+            nc.scalar.activation(tok_bf[:, piece * PIECE : (piece + 1) * PIECE], tok[:], ACT.Copy)
             nc.vector.tensor_reduce(
-                sq_sum[:, half * EH : (half + 1) * EH], by_entity(squares[half][:]), X, ALU.add
+                sq_sum[:, ents], squares[:].rearrange("r (e t) -> r e t", t=L), X, ALU.add
             )
 
-        sum_of_squares(0)
-        sum_of_squares(1)
+        def extreme(half, op, result, label):
+            ents = HALF // L
+            cur = tok_bf[:, half * HALF : (half + 1) * HALF].rearrange("r (e t) -> r e t", t=L)
+            width = L // 2
+            while width > 1:
+                nxt = held.tile([P, ents, width], BF16, name=f"{label}{half}_{width}")
+                nc.vector.tensor_tensor(nxt[:], cur[:, :, 0:width], cur[:, :, width : 2 * width], op)
+                cur = nxt[:]
+                width //= 2
+            last = result[:, half * ents : (half + 1) * ents].unsqueeze(2)
+            nc.vector.tensor_tensor(last, cur[:, :, 0:1], cur[:, :, 1:2], op)
+
+        sums(0)
+        sums(1)
+        extreme(0, ALU.max, max_bf, "max")
+        extreme(0, ALU.min, min_bf, "min")
+        sums(2)
+        sums(3)
 
         nc.scalar.activation(mean_bf[:], tok_sum[:], ACT.Copy, scale=1.0 / L)
         sum2_over_l = held.tile([P, B], F32, name="sum2_over_l")
         nc.scalar.activation(sum2_over_l[:], tok_sum[:], ACT.Square, scale=0.25)
         spread = held.tile([P, B], F32, name="spread")
-        nc.vector.tensor_tensor(spread[:], sq_sum[:], sum2_over_l[:], ALU.max)
-        nc.vector.tensor_tensor(spread[:], spread[:], sum2_over_l[:], ALU.subtract)
-        nc.scalar.activation(sd_bf[:], spread[:], ACT.Sqrt, scale=1.0 / L)
+        nc.vector.tensor_tensor(spread[:], sq_sum[:], sum2_over_l[:], ALU.subtract)
+        variance = held.tile([P, B], F32, name="variance")
+        nc.scalar.activation(variance[:], spread[:], ACT.Relu, scale=1.0 / L)
+        nc.scalar.activation(sd_bf[:], variance[:], ACT.Sqrt)
+        second_set = held.tile([P, 1], F32, name="second_set")
+        nc.scalar.activation(
+            second_set[:], sd_bf[:, 0:1], ACT.Abs_reciprocal_sqrt, bias=1.0, scale=0.0
+        )
 
-        chains = [
-            (op, result, label, half)
-            for half in range(HALVES)
-            for op, result, label in ((ALU.max, max_bf, "max"), (ALU.min, min_bf, "min"))
-        ]
-        cur = [by_entity(tok_bf[half][:]) for op, result, label, half in chains]
-        width = L // 2
-        while width >= 1:
-            for c, (op, result, label, half) in enumerate(chains):
-                if width > 1:
-                    nxt = held.tile([P, EH, width], BF16, name=f"{label}{half}_{width}")[:]
-                else:
-                    nxt = result[:, half * EH : (half + 1) * EH].unsqueeze(2)
-                nc.vector.tensor_tensor(
-                    nxt, cur[c][:, :, 0:width], cur[c][:, :, width : 2 * width], op
-                )
-                cur[c] = nxt
-            width //= 2
+        extreme(1, ALU.max, max_bf, "max")
+        extreme(1, ALU.min, min_bf, "min")
 
         blocks = [(a, t) for a in (0, 3, 1, 2) for t in range(SCALERS)]
         for i, (a, t) in enumerate(blocks):
@@ -126,10 +123,8 @@ def tile_basepnaretriever_kernel(tc, table, w_down, w_re, b_re, offs, out):
         res_squared = held.tile([P, R], F32, name="res_squared")
         length2 = held.tile([P, 1], F32, name="length2")
         nc.scalar.activation(res_squared[:], res_ps[:], ACT.Square, accum_out=length2[:])
-        length = held.tile([P, 1], F32, name="length")
-        nc.scalar.activation(length[:], length2[:], ACT.Sqrt)
         inv_length = held.tile([P, 1], F32, name="inv_length")
-        nc.vector.reciprocal(inv_length[:], length[:])
+        nc.scalar.activation(inv_length[:], length2[:], ACT.Abs_reciprocal_sqrt)
         unit = held.tile([P, R], F32, name="unit")
-        nc.vector.tensor_scalar(unit[:], res_ps[:], inv_length[:], None, ALU.mult)
-        nc.sync.dma_start(out, unit[:])
+        nc.scalar.activation(unit[:], res_ps[:], ACT.Copy, scale=inv_length[:])
+        nc.scalar.dma_start(out, unit[:])

@@ -20,8 +20,6 @@ AGGS = 4
 SCALERS = 3
 
 FLOPS = 2 * P * R * N + 2 * SCALERS * AGGS * R * B * R
-HALF = N // 2
-HALVES = N // HALF
 
 
 def tile_basepnaretriever_kernel(tc, table, w_down, w_re, b_re, offs, out):
@@ -75,24 +73,8 @@ def tile_basepnaretriever_kernel(tc, table, w_down, w_re, b_re, offs, out):
                 sq_sum[:, ents], squares[:].rearrange("r (e t) -> r e t", t=L), X, ALU.add
             )
 
-        def extreme(half, op, result, label):
-            ents = HALF // L
-            cur = tok_bf[:, half * HALF : (half + 1) * HALF].rearrange("r (e t) -> r e t", t=L)
-            width = L // 2
-            while width > 1:
-                nxt = held.tile([P, ents, width], BF16, name=f"{label}{half}_{width}")
-                nc.vector.tensor_tensor(nxt[:], cur[:, :, 0:width], cur[:, :, width : 2 * width], op)
-                cur = nxt[:]
-                width //= 2
-            last = result[:, half * ents : (half + 1) * ents].unsqueeze(2)
-            nc.vector.tensor_tensor(last, cur[:, :, 0:1], cur[:, :, 1:2], op)
-
-        sums(0)
-        sums(1)
-        extreme(0, ALU.max, max_bf, "max")
-        extreme(0, ALU.min, min_bf, "min")
-        sums(2)
-        sums(3)
+        for piece in range(PIECES):
+            sums(piece)
 
         nc.scalar.activation(mean_bf[:], tok_sum[:], ACT.Copy, scale=1.0 / L)
         sum2_over_l = held.tile([P, B], F32, name="sum2_over_l")
@@ -107,8 +89,20 @@ def tile_basepnaretriever_kernel(tc, table, w_down, w_re, b_re, offs, out):
             second_set[:], sd_bf[:, 0:1], ACT.Abs_reciprocal_sqrt, bias=1.0, scale=0.0
         )
 
-        extreme(1, ALU.max, max_bf, "max")
-        extreme(1, ALU.min, min_bf, "min")
+        extremes = (("max", ALU.max, max_bf), ("min", ALU.min, min_bf))
+        cur = {label: tok_bf[:].rearrange("r (e t) -> r e t", t=L) for label, op, result in extremes}
+        width = L // 2
+        while width >= 1:
+            for label, op, result in extremes:
+                if width > 1:
+                    nxt = held.tile([P, B, width], BF16, name=f"{label}_{width}")[:]
+                else:
+                    nxt = result[:].unsqueeze(2)
+                nc.vector.tensor_tensor(
+                    nxt, cur[label][:, :, 0:width], cur[label][:, :, width : 2 * width], op
+                )
+                cur[label] = nxt
+            width //= 2
 
         blocks = [(a, t) for a in (0, 3, 1, 2) for t in range(SCALERS)]
         for i, (a, t) in enumerate(blocks):

@@ -73,8 +73,29 @@ def tile_basepnaretriever_kernel(tc, table, w_down, w_re, b_re, offs, out):
                 sq_sum[:, ents], squares[:].rearrange("r (e t) -> r e t", t=L), X, ALU.add
             )
 
-        for piece in range(PIECES):
-            sums(piece)
+        def extremes(first, last):
+            ents = (last - first) * E
+            both = (("max", ALU.max, max_bf), ("min", ALU.min, min_bf))
+            start = tok_bf[:, first * PIECE : last * PIECE].rearrange("r (e t) -> r e t", t=L)
+            cur = {label: start for label, op, result in both}
+            width = L // 2
+            while width >= 1:
+                for label, op, result in both:
+                    if width > 1:
+                        nxt = held.tile([P, ents, width], BF16, name=f"{label}{first}_{width}")[:]
+                    else:
+                        nxt = result[:, first * E : last * E].unsqueeze(2)
+                    nc.vector.tensor_tensor(
+                        nxt, cur[label][:, :, 0:width], cur[label][:, :, width : 2 * width], op
+                    )
+                    cur[label] = nxt
+                width //= 2
+
+        sums(0)
+        sums(1)
+        extremes(0, 2)
+        sums(2)
+        sums(3)
 
         nc.scalar.activation(mean_bf[:], tok_sum[:], ACT.Copy, scale=1.0 / L)
         sum2_over_l = held.tile([P, B], F32, name="sum2_over_l")
@@ -89,20 +110,7 @@ def tile_basepnaretriever_kernel(tc, table, w_down, w_re, b_re, offs, out):
             second_set[:], sd_bf[:, 0:1], ACT.Abs_reciprocal_sqrt, bias=1.0, scale=0.0
         )
 
-        extremes = (("max", ALU.max, max_bf), ("min", ALU.min, min_bf))
-        cur = {label: tok_bf[:].rearrange("r (e t) -> r e t", t=L) for label, op, result in extremes}
-        width = L // 2
-        while width >= 1:
-            for label, op, result in extremes:
-                if width > 1:
-                    nxt = held.tile([P, B, width], BF16, name=f"{label}_{width}")[:]
-                else:
-                    nxt = result[:].unsqueeze(2)
-                nc.vector.tensor_tensor(
-                    nxt, cur[label][:, :, 0:width], cur[label][:, :, width : 2 * width], op
-                )
-                cur[label] = nxt
-            width //= 2
+        extremes(2, 4)
 
         blocks = [(a, t) for a in (0, 3, 1, 2) for t in range(SCALERS)]
         for i, (a, t) in enumerate(blocks):

@@ -18,6 +18,7 @@ PIECES = N // PIECE
 E = PIECE // L
 AGGS = 4
 SCALERS = 3
+TINY = 1e-36
 
 FLOPS = 2 * P * R * N + 2 * SCALERS * AGGS * R * B * R
 
@@ -43,7 +44,7 @@ def tile_basepnaretriever_kernel(tc, table, w_down, w_re, b_re, offs, out):
         nc.gpsimd.memset(ones[:], 1.0)
 
         first_set = held.tile([P, 1], F32, name="first_set")
-        nc.scalar.activation(first_set[:], ones[:, 0:1], ACT.Sqrt)
+        nc.scalar.activation(first_set[:], ones[:, 0:1], ACT.Abs_reciprocal_sqrt)
 
         tok_sum = held.tile([P, B], F32, name="tok_sum")
         sq_sum = held.tile([P, B], F32, name="sq_sum")
@@ -102,13 +103,11 @@ def tile_basepnaretriever_kernel(tc, table, w_down, w_re, b_re, offs, out):
         nc.scalar.activation(sum2_over_l[:], tok_sum[:], ACT.Square, scale=0.25)
         spread = held.tile([P, B], F32, name="spread")
         nc.vector.tensor_tensor(spread[:], sq_sum[:], sum2_over_l[:], ALU.subtract)
-        variance = held.tile([P, B], F32, name="variance")
-        nc.scalar.activation(variance[:], spread[:], ACT.Relu, scale=1.0 / L)
-        nc.scalar.activation(sd_bf[:], variance[:], ACT.Sqrt)
-        second_set = held.tile([P, 1], F32, name="second_set")
+        inv_root = held.tile([P, B], F32, name="inv_root")
         nc.scalar.activation(
-            second_set[:], sd_bf[:, 0:1], ACT.Abs_reciprocal_sqrt, bias=1.0, scale=0.0
+            inv_root[:], spread[:], ACT.Abs_reciprocal_sqrt, bias=TINY, scale=float(L)
         )
+        nc.vector.scalar_tensor_tensor(sd_bf[:], spread[:], 0.0, inv_root[:], ALU.max, ALU.mult)
 
         extremes(2, 4)
 

@@ -18,6 +18,8 @@ PIECES = N // PIECE
 E = PIECE // L
 AGGS = 4
 SCALERS = 3
+HALVES = 2
+HALF_ENTS = B // HALVES
 TINY = 1e-36
 
 FLOPS = 2 * P * R * N + 2 * SCALERS * AGGS * R * B * R
@@ -48,7 +50,7 @@ def tile_basepnaretriever_kernel(tc, table, w_down, w_re, b_re, offs, out):
 
         tok_sum = held.tile([P, B], F32, name="tok_sum")
         sq_sum = held.tile([P, B], F32, name="sq_sum")
-        tok_bf = held.tile([P, N], BF16, name="tok_bf")
+        tok_bf = [held.tile([P, L, HALF_ENTS], BF16, name=f"tok_bf{half}") for half in range(HALVES)]
         feat = [held.tile([P, B], BF16, name=f"feat{a}") for a in range(AGGS)]
         mean_bf, max_bf, min_bf, sd_bf = feat
 
@@ -69,32 +71,35 @@ def tile_basepnaretriever_kernel(tc, table, w_down, w_re, b_re, offs, out):
             )
             squares = held.tile([P, PIECE], F32, name=f"squares{piece}")
             nc.scalar.activation(squares[:], tok[:], ACT.Square)
-            nc.scalar.activation(tok_bf[:, piece * PIECE : (piece + 1) * PIECE], tok[:], ACT.Copy)
+            half, place = divmod(piece, PIECES // HALVES)
+            nc.scalar.activation(
+                tok_bf[half][:, :, place * E : (place + 1) * E],
+                tok[:].rearrange("r (e t) -> r t e", t=L),
+                ACT.Copy,
+            )
             nc.vector.tensor_reduce(
                 sq_sum[:, ents], squares[:].rearrange("r (e t) -> r e t", t=L), X, ALU.add
             )
 
-        def extremes(first, last):
-            ents = (last - first) * E
+        def extremes(half):
             both = (("max", ALU.max, max_bf), ("min", ALU.min, min_bf))
-            start = tok_bf[:, first * PIECE : last * PIECE].rearrange("r (e t) -> r e t", t=L)
-            cur = {label: start for label, op, result in both}
+            cur = {label: tok_bf[half][:] for label, op, result in both}
             width = L // 2
             while width >= 1:
                 for label, op, result in both:
                     if width > 1:
-                        nxt = held.tile([P, ents, width], BF16, name=f"{label}{first}_{width}")[:]
+                        nxt = held.tile([P, width, HALF_ENTS], BF16, name=f"{label}{half}_{width}")[:]
                     else:
-                        nxt = result[:, first * E : last * E].unsqueeze(2)
+                        nxt = result[:, half * HALF_ENTS : (half + 1) * HALF_ENTS].unsqueeze(1)
                     nc.vector.tensor_tensor(
-                        nxt, cur[label][:, :, 0:width], cur[label][:, :, width : 2 * width], op
+                        nxt, cur[label][:, 0:width, :], cur[label][:, width : 2 * width, :], op
                     )
                     cur[label] = nxt
                 width //= 2
 
         sums(0)
         sums(1)
-        extremes(0, 2)
+        extremes(0)
         sums(2)
         sums(3)
 
@@ -109,7 +114,7 @@ def tile_basepnaretriever_kernel(tc, table, w_down, w_re, b_re, offs, out):
         )
         nc.vector.scalar_tensor_tensor(sd_bf[:], spread[:], 0.0, inv_root[:], ALU.max, ALU.mult)
 
-        extremes(2, 4)
+        extremes(1)
 
         blocks = [(a, t) for a in (0, 3, 1, 2) for t in range(SCALERS)]
         for i, (a, t) in enumerate(blocks):

@@ -13,9 +13,9 @@ N = 2048
 L = 16
 B = N // L
 R = 128
-PIECE = 512
-PIECES = N // PIECE
-E = PIECE // L
+BANK = 512
+CUTS = (0, 8, 32, 64, 96, 128)
+PIECES = len(CUTS) - 1
 AGGS = 4
 SCALERS = 3
 HALVES = 2
@@ -56,29 +56,32 @@ def tile_basepnaretriever_kernel(tc, table, w_down, w_re, b_re, offs, out):
 
         toks = []
         for piece in range(PIECES):
-            tok = psum.tile([P, PIECE], F32, name=f"tok{piece}")
-            picked = table_sb[:].indirect(offsets[:, piece * E : (piece + 1) * E])
-            nc.tensor.matmul(tok[:], w_down_sb[:], picked, start=True, stop=True)
+            first, last = CUTS[piece], CUTS[piece + 1]
+            bank = psum.tile([P, BANK], F32, name=f"tok{piece}")
+            tok = bank[:, 0 : (last - first) * L]
+            nc.tensor.matmul(
+                tok, w_down_sb[:], table_sb[:].indirect(offsets[:, first:last]), start=True, stop=True
+            )
             toks.append(tok)
         res_ps = psum.tile([P, R], F32, name="res_ps")
         nc.tensor.matmul(res_ps[:], ones[:], bias_rows[:], start=True, stop=False)
 
         def sums(piece):
-            ents = slice(piece * E, (piece + 1) * E)
+            first, last = CUTS[piece], CUTS[piece + 1]
             tok = toks[piece]
             nc.vector.tensor_reduce(
-                tok_sum[:, ents], tok[:].rearrange("r (e t) -> r e t", t=L), X, ALU.add
+                tok_sum[:, first:last], tok.rearrange("r (e t) -> r e t", t=L), X, ALU.add
             )
-            squares = held.tile([P, PIECE], F32, name=f"squares{piece}")
-            nc.scalar.activation(squares[:], tok[:], ACT.Square)
-            half, place = divmod(piece, PIECES // HALVES)
+            squares = held.tile([P, (last - first) * L], F32, name=f"squares{piece}")
+            nc.scalar.activation(squares[:], tok, ACT.Square)
+            half = first // HALF_ENTS
             nc.scalar.activation(
-                tok_bf[half][:, :, place * E : (place + 1) * E],
-                tok[:].rearrange("r (e t) -> r t e", t=L),
+                tok_bf[half][:, :, first - half * HALF_ENTS : last - half * HALF_ENTS],
+                tok.rearrange("r (e t) -> r t e", t=L),
                 ACT.Copy,
             )
             nc.vector.tensor_reduce(
-                sq_sum[:, ents], squares[:].rearrange("r (e t) -> r e t", t=L), X, ALU.add
+                sq_sum[:, first:last], squares[:].rearrange("r (e t) -> r e t", t=L), X, ALU.add
             )
 
         def extremes(half):
@@ -97,11 +100,10 @@ def tile_basepnaretriever_kernel(tc, table, w_down, w_re, b_re, offs, out):
                     cur[label] = nxt
                 width //= 2
 
-        sums(0)
-        sums(1)
-        extremes(0)
-        sums(2)
-        sums(3)
+        for piece in range(PIECES):
+            sums(piece)
+            if CUTS[piece + 1] == HALF_ENTS:
+                extremes(0)
 
         nc.scalar.activation(mean_bf[:], tok_sum[:], ACT.Copy, scale=1.0 / L)
         sum2_over_l = held.tile([P, B], F32, name="sum2_over_l")

@@ -20,6 +20,7 @@ AGGS = 4
 SCALERS = 3
 HALVES = 2
 HALF_ENTS = B // HALVES
+WIDTHS = (8, 4, 2, 1)
 TINY = 1e-36
 
 FLOPS = 2 * P * R * N + 2 * SCALERS * AGGS * R * B * R
@@ -84,21 +85,21 @@ def tile_basepnaretriever_kernel(tc, table, w_down, w_re, b_re, offs, out):
                 sq_sum[:, first:last], squares[:].rearrange("r (e t) -> r e t", t=L), X, ALU.add
             )
 
+        def halve(label, op, result, half, cur, width):
+            if width > 1:
+                nxt = held.tile([P, width, HALF_ENTS], BF16, name=f"{label}{half}_{width}")[:]
+            else:
+                nxt = result[:, half * HALF_ENTS : (half + 1) * HALF_ENTS].unsqueeze(1)
+            nc.vector.tensor_tensor(nxt, cur[:, 0:width, :], cur[:, width : 2 * width, :], op)
+            return nxt
+
         def extremes(half):
-            both = (("max", ALU.max, max_bf), ("min", ALU.min, min_bf))
-            cur = {label: tok_bf[half][:] for label, op, result in both}
-            width = L // 2
-            while width >= 1:
-                for label, op, result in both:
-                    if width > 1:
-                        nxt = held.tile([P, width, HALF_ENTS], BF16, name=f"{label}{half}_{width}")[:]
-                    else:
-                        nxt = result[:, half * HALF_ENTS : (half + 1) * HALF_ENTS].unsqueeze(1)
-                    nc.vector.tensor_tensor(
-                        nxt, cur[label][:, 0:width, :], cur[label][:, width : 2 * width, :], op
-                    )
-                    cur[label] = nxt
-                width //= 2
+            cur_max = cur_min = tok_bf[half][:]
+            for step in range(len(WIDTHS) + 1):
+                if step < len(WIDTHS):
+                    cur_max = halve("max", ALU.max, max_bf, half, cur_max, WIDTHS[step])
+                if step > 0:
+                    cur_min = halve("min", ALU.min, min_bf, half, cur_min, WIDTHS[step - 1])
 
         for piece in range(PIECES):
             sums(piece)

@@ -18,6 +18,9 @@ CUTS = (0, 8, 32, 64, 96, 128)
 PIECES = len(CUTS) - 1
 AGGS = 4
 SCALERS = 3
+BLOCK = 32
+QUARTERS = 4
+QUARTER = L // QUARTERS
 HALVES = 2
 HALF_ENTS = B // HALVES
 WIDTHS = (8, 4, 2, 1)
@@ -44,13 +47,28 @@ def tile_basepnaretriever_kernel(tc, table, w_down, w_re, b_re, offs, out):
         nc.gpsimd.memset(bias_rows[:], 0.0)
         nc.sync.dma_start(bias_rows[0:1, :], b_re.rearrange("r o -> o r"))
         ones = held.tile([P, B], F32, name="ones")
-        nc.gpsimd.memset(ones[:], 1.0)
+        nc.vector.memset(ones[:], 1.0)
+
+        columns = held.tile([P, BLOCK], F32, name="columns", align_bytes=64)
+        nc.vector.tensor_tensor_scan(
+            columns[:], ones[:, 0:BLOCK], ones[:, 0:BLOCK], 0.0, ALU.mult, ALU.add
+        )
+        rows = held.tile([P, BLOCK], F32, name="rows", align_bytes=64)
+        nc.vector.transpose(rows[:], columns[:])
+        identity = held.tile([P, P], F32, name="identity")
+        nc.gpsimd.memset(identity[:], 0.0)
+        for start in range(0, P, BLOCK):
+            block = slice(start, start + BLOCK)
+            nc.vector.tensor_tensor(
+                identity[block, block], rows[block, :], columns[block, :], ALU.is_equal
+            )
 
         first_set = held.tile([P, 1], F32, name="first_set")
         nc.scalar.activation(first_set[:], ones[:, 0:1], ACT.Abs_reciprocal_sqrt)
 
         tok_sum = held.tile([P, B], F32, name="tok_sum")
         sq_sum = held.tile([P, B], F32, name="sq_sum")
+        squares = held.tile([P, B, L], F32, name="squares")
         tok_bf = [held.tile([P, L, HALF_ENTS], BF16, name=f"tok_bf{half}") for half in range(HALVES)]
         feat = [held.tile([P, B], BF16, name=f"feat{a}") for a in range(AGGS)]
         mean_bf, max_bf, min_bf, sd_bf = feat
@@ -73,17 +91,29 @@ def tile_basepnaretriever_kernel(tc, table, w_down, w_re, b_re, offs, out):
             nc.vector.tensor_reduce(
                 tok_sum[:, first:last], tok.rearrange("r (e t) -> r e t", t=L), X, ALU.add
             )
-            squares = held.tile([P, (last - first) * L], F32, name=f"squares{piece}")
-            nc.scalar.activation(squares[:], tok, ACT.Square)
+            nc.scalar.activation(
+                squares[:, first:last, :], tok.rearrange("r (e t) -> r e t", t=L), ACT.Square
+            )
             half = first // HALF_ENTS
             nc.scalar.activation(
                 tok_bf[half][:, :, first - half * HALF_ENTS : last - half * HALF_ENTS],
                 tok.rearrange("r (e t) -> r t e", t=L),
                 ACT.Copy,
             )
-            nc.vector.tensor_reduce(
-                sq_sum[:, first:last], squares[:].rearrange("r (e t) -> r e t", t=L), X, ALU.add
-            )
+            if first >= HALF_ENTS:
+                nc.vector.tensor_reduce(sq_sum[:, first:last], squares[:, first:last, :], X, ALU.add)
+
+        def first_half_square_sums():
+            quarters = psum.tile([P, HALF_ENTS, QUARTER], F32, name="quarters")
+            for q in range(QUARTERS):
+                nc.tensor.matmul(
+                    quarters[:],
+                    identity[:],
+                    squares[:, 0:HALF_ENTS, q * QUARTER : (q + 1) * QUARTER],
+                    start=(q == 0),
+                    stop=(q == QUARTERS - 1),
+                )
+            nc.vector.tensor_reduce(sq_sum[:, 0:HALF_ENTS], quarters[:], X, ALU.add)
 
         def halve(label, op, result, half, cur, width):
             if width > 1:
@@ -105,6 +135,7 @@ def tile_basepnaretriever_kernel(tc, table, w_down, w_re, b_re, offs, out):
             sums(piece)
             if CUTS[piece + 1] == HALF_ENTS:
                 extremes(0)
+                first_half_square_sums()
 
         nc.scalar.activation(mean_bf[:], tok_sum[:], ACT.Copy, scale=1.0 / L)
         sum2_over_l = held.tile([P, B], F32, name="sum2_over_l")

import concourse.mybir as mybir

F32 = mybir.dt.float32
BF16 = mybir.dt.bfloat16
U16 = mybir.dt.uint16
ALU = mybir.AluOpType
ACT = mybir.ActivationFunctionType
X = mybir.AxisListType.X

P = 128
S = 1024
N = 2048
L = 16
B = N // L
R = 128
BANK = 512
CUTS = (0, 8, 32, 64, 96, 128)
PIECES = len(CUTS) - 1
AGGS = 4
SCALERS = 3
BLOCK = 32
QUARTERS = 4
QUARTER = L // QUARTERS
HALVES = 2
HALF_ENTS = B // HALVES
WIDTHS = (8, 4, 2, 1)
TINY = 1e-36

FLOPS = 2 * P * R * N + 2 * SCALERS * AGGS * R * B * R


def tile_basepnaretriever_kernel(tc, table, w_down, w_re, b_re, offs, out):
    nc = tc.nc
    with (
        tc.tile_pool(name="held", bufs=1) as held,
        tc.psum_pool(name="psum", bufs=1) as psum,
    ):
        offsets = held.tile([P, N // 16], U16, name="offsets")
        nc.sync.dma_start(offsets[:], offs)
        table_sb = held.tile([P, S], BF16, name="table_sb")
        nc.scalar.dma_start(table_sb[:], table)
        w_down_sb = held.tile([P, R], BF16, name="w_down_sb")
        nc.sync.dma_start(w_down_sb[:], w_down)
        w_re_sb = held.tile([P, SCALERS * AGGS, R], BF16, name="w_re_sb")
        nc.sync.dma_start(w_re_sb[:], w_re.rearrange("(c f) r -> f c r", f=P))
        bias_rows = held.tile([P, R], F32, name="bias_rows")
        nc.gpsimd.memset(bias_rows[:], 0.0)
        nc.sync.dma_start(bias_rows[0:1, :], b_re.rearrange("r o -> o r"))
        ones = held.tile([P, B], F32, name="ones")
        nc.vector.memset(ones[:], 1.0)

        columns = held.tile([P, BLOCK], F32, name="columns", align_bytes=64)
        nc.vector.tensor_tensor_scan(
            columns[:], ones[:, 0:BLOCK], ones[:, 0:BLOCK], 0.0, ALU.mult, ALU.add
        )
        rows = held.tile([P, BLOCK], F32, name="rows", align_bytes=64)
        nc.vector.transpose(rows[:], columns[:])
        identity = held.tile([P, P], F32, name="identity")
        nc.gpsimd.memset(identity[:], 0.0)
        for start in range(0, P, BLOCK):
            block = slice(start, start + BLOCK)
            nc.vector.tensor_tensor(
                identity[block, block], rows[block, :], columns[block, :], ALU.is_equal
            )

        first_set = held.tile([P, 1], F32, name="first_set")
        nc.scalar.activation(first_set[:], ones[:, 0:1], ACT.Abs_reciprocal_sqrt)

        tok_sum = held.tile([P, B], F32, name="tok_sum")
        sq_sum = held.tile([P, B], F32, name="sq_sum")
        squares = held.tile([P, B, L], F32, name="squares")
        tok_bf = [held.tile([P, L, HALF_ENTS], BF16, name=f"tok_bf{half}") for half in range(HALVES)]
        feat = [held.tile([P, B], BF16, name=f"feat{a}") for a in range(AGGS)]
        mean_bf, max_bf, min_bf, sd_bf = feat

        toks = []
        for piece in range(PIECES):
            first, last = CUTS[piece], CUTS[piece + 1]
            bank = psum.tile([P, BANK], F32, name=f"tok{piece}")
            tok = bank[:, 0 : (last - first) * L]
            nc.tensor.matmul(
                tok, w_down_sb[:], table_sb[:].indirect(offsets[:, first:last]), start=True, stop=True
            )
            toks.append(tok)
        res_ps = psum.tile([P, R], F32, name="res_ps")
        nc.tensor.matmul(res_ps[:], ones[:], bias_rows[:], start=True, stop=False)

        def sums(piece):
            first, last = CUTS[piece], CUTS[piece + 1]
            tok = toks[piece]
            nc.vector.tensor_reduce(
                tok_sum[:, first:last], tok.rearrange("r (e t) -> r e t", t=L), X, ALU.add
            )
            nc.scalar.activation(
                squares[:, first:last, :], tok.rearrange("r (e t) -> r e t", t=L), ACT.Square
            )
            half = first // HALF_ENTS
            nc.scalar.activation(
                tok_bf[half][:, :, first - half * HALF_ENTS : last - half * HALF_ENTS],
                tok.rearrange("r (e t) -> r t e", t=L),
                ACT.Copy,
            )
            if first >= HALF_ENTS:
                nc.vector.tensor_reduce(sq_sum[:, first:last], squares[:, first:last, :], X, ALU.add)

        def first_half_square_sums():
            quarters = psum.tile([P, HALF_ENTS, QUARTER], F32, name="quarters")
            for q in range(QUARTERS):
                nc.tensor.matmul(
                    quarters[:],
                    identity[:],
                    squares[:, 0:HALF_ENTS, q * QUARTER : (q + 1) * QUARTER],
                    start=(q == 0),
                    stop=(q == QUARTERS - 1),
                )
            nc.vector.tensor_reduce(sq_sum[:, 0:HALF_ENTS], quarters[:], X, ALU.add)

        def halve(label, op, result, half, cur, width):
            if width > 1:
                nxt = held.tile([P, width, HALF_ENTS], BF16, name=f"{label}{half}_{width}")[:]
            else:
                nxt = result[:, half * HALF_ENTS : (half + 1) * HALF_ENTS].unsqueeze(1)
            nc.vector.tensor_tensor(nxt, cur[:, 0:width, :], cur[:, width : 2 * width, :], op)
            return nxt

        def extremes(half):
            cur_max = cur_min = tok_bf[half][:]
            for step in range(len(WIDTHS) + 1):
                if step < len(WIDTHS):
                    cur_max = halve("max", ALU.max, max_bf, half, cur_max, WIDTHS[step])
                if step > 0:
                    cur_min = halve("min", ALU.min, min_bf, half, cur_min, WIDTHS[step - 1])

        for piece in range(PIECES):
            sums(piece)
            if CUTS[piece + 1] == HALF_ENTS:
                extremes(0)
                first_half_square_sums()

        nc.scalar.activation(mean_bf[:], tok_sum[:], ACT.Copy, scale=1.0 / L)
        sum2_over_l = held.tile([P, B], F32, name="sum2_over_l")
        nc.scalar.activation(sum2_over_l[:], tok_sum[:], ACT.Square, scale=0.25)
        spread = held.tile([P, B], F32, name="spread")
        nc.vector.tensor_tensor(spread[:], sq_sum[:], sum2_over_l[:], ALU.subtract)
        inv_root = held.tile([P, B], F32, name="inv_root")
        nc.scalar.activation(
            inv_root[:], spread[:], ACT.Abs_reciprocal_sqrt, bias=TINY, scale=float(L)
        )
        nc.vector.scalar_tensor_tensor(sd_bf[:], spread[:], 0.0, inv_root[:], ALU.max, ALU.mult)

        extremes(1)

        blocks = [(a, t) for a in (0, 3, 1, 2) for t in range(SCALERS)]
        for i, (a, t) in enumerate(blocks):
            nc.tensor.matmul(
                res_ps[:],
                feat[a][:],
                w_re_sb[:, t * AGGS + a, :],
                start=False,
                stop=(i == len(blocks) - 1),
            )

        res_squared = held.tile([P, R], F32, name="res_squared")
        length2 = held.tile([P, 1], F32, name="length2")
        nc.scalar.activation(res_squared[:], res_ps[:], ACT.Square, accum_out=length2[:])
        inv_length = held.tile([P, 1], F32, name="inv_length")
        nc.scalar.activation(inv_length[:], length2[:], ACT.Abs_reciprocal_sqrt)
        unit = held.tile([P, R], F32, name="unit")
        nc.scalar.activation(unit[:], res_ps[:], ACT.Copy, scale=inv_length[:])
        nc.scalar.dma_start(out, unit[:])
